import numpy as np
import ml_dtypes

BF16 = ml_dtypes.bfloat16


def bf(x):
    return np.asarray(x, np.float32).astype(BF16)


def f32(x):
    return np.asarray(x, np.float32)


def f64(x):
    return np.asarray(x).astype(np.float64)


def striped(idx):
    return np.tile(idx.reshape(-1, 16).T, (8, 1))


D, S, N, H, R, T, NK, OP = 1024, 2048, 3072, 1024, 3, 128, 4, 256


def setup_inputs():
    x = f32(0.125 * np.random.standard_normal((D, S)))
    rel = f32(np.random.uniform(0.0, 1.0, (T, N)))
    mean_rel = f32((np.arange(NK) + np.random.uniform(0.0, 1.0, NK)).reshape(1, NK) / NK)
    prec_rel = f32(0.3 + 0.4 * np.random.uniform(0.0, 1.0, (1, NK)))
    w = bf(np.random.uniform(-1.0, 1.0, (D, NK * OP)) / np.sqrt(D))
    idx = np.concatenate([np.random.permutation(S)[:H] for _ in range(R)])
    return {"x": x, "rel": rel, "mean_rel": mean_rel, "prec_rel": prec_rel, "w": w, "offs": striped(idx)}


def reference(x, rel, mean_rel, prec_rel, w, offs):
    idx = offs[:16].T.reshape(-1)
    r = f64(rel)[None, :, :]
    mu = f64(mean_rel).reshape(NK, 1, 1)
    p = f64(prec_rel).reshape(NK, 1, 1)
    e = np.exp(-0.5 * (r - mu) ** 2 / p ** 2)
    u = e / e.sum(axis=0, keepdims=True)
    ws = u.sum(axis=1)
    xg = f64(x)[:, idx]
    wk = f64(w)
    return np.concatenate([wk[:, n * OP:(n + 1) * OP].T @ (xg * ws[n][None, :]) for n in range(NK)], axis=0)

@@ -1,0 +1,128 @@
+import math
+
+import concourse.mybir as mybir
+
+F32 = mybir.dt.float32
+BF16 = mybir.dt.bfloat16
+U16 = mybir.dt.uint16
+ALU = mybir.AluOpType
+ACT = mybir.ActivationFunctionType
+
+P = 128
+D, S, N = 1024, 2048, 3072
+NK, OP = 4, 256
+D_BLOCKS = D // P
+O_BLOCKS = OP // P
+PIECE = 1024
+BANK = 512
+BANKS = PIECE // BANK
+
+FLOPS = 2 * D * NK * OP * N
+
+
+def tile_visualconvolution_b_kernel(tc, x, rel, mean_rel, prec_rel, w, offs, out):
+    nc = tc.nc
+    with (
+        tc.tile_pool(name="held", bufs=1) as held,
+        tc.tile_pool(name="weights", bufs=2) as weights,
+        tc.tile_pool(name="soft", bufs=1) as soft,
+        tc.tile_pool(name="products", bufs=4) as products,
+        tc.tile_pool(name="staging", bufs=3) as staging,
+        tc.psum_pool(name="sums", bufs=2) as sums,
+        tc.psum_pool(name="accs", bufs=6) as accs,
+    ):
+        offsets = held.tile([P, N // 16], U16, name="offsets")
+        nc.sync.dma_start(offsets[:], offs)
+        mean_all = held.tile([P, NK], F32, name="mean_all")
+        nc.sync.dma_start(mean_all[:], mean_rel.broadcast_to([P, NK]))
+        width_all = held.tile([P, NK], F32, name="width_all")
+        nc.sync.dma_start(width_all[:], prec_rel.broadcast_to([P, NK]))
+        rel_sb = held.tile([P, N], F32, name="rel_sb")
+        nc.sync.dma_start(rel_sb[:, 0:PIECE], rel[:, 0:PIECE])
+        x_blocks = [held.tile([P, S], F32, name=f"x{b}") for b in range(D_BLOCKS)]
+        w_sb = held.tile([P, D_BLOCKS, NK * OP], BF16, name="w_sb")
+        for b in range(D_BLOCKS):
+            nc.sync.dma_start(x_blocks[b][:], x[b * P : (b + 1) * P, :])
+            nc.sync.dma_start(w_sb[:, b, :], w[b * P : (b + 1) * P, :])
+        nc.sync.dma_start(rel_sb[:, PIECE:N], rel[:, PIECE:N])
+
+        ones = held.tile([P, P], BF16, name="ones")
+        nc.gpsimd.memset(ones[:], 1.0)
+        inv_width = held.tile([P, NK], F32, name="inv_width")
+        nc.vector.reciprocal(inv_width[:], width_all[:])
+        slope = held.tile([P, NK], F32, name="slope")
+        nc.vector.tensor_scalar_mul(slope[:], inv_width[:], math.sqrt(0.5))
+        neg_mean = held.tile([P, NK], F32, name="neg_mean")
+        nc.vector.tensor_scalar_mul(neg_mean[:], mean_all[:], -1.0)
+        shift = held.tile([P, NK], F32, name="shift")
+        nc.vector.tensor_tensor(shift[:], neg_mean[:], slope[:], ALU.mult)
+
+        def relation_weights(piece):
+            rel_piece = rel_sb[:, piece * PIECE : (piece + 1) * PIECE]
+            dist = soft.tile([P, NK, PIECE], F32, name="dist")
+            for n in range(NK):
+                nc.scalar.activation(
+                    dist[:, n, :], rel_piece, ACT.Square, bias=shift[:, n : n + 1], scale=slope[:, n : n + 1]
+                )
+            nearest = soft.tile([P, PIECE], F32, name="nearest")
+            nc.vector.tensor_tensor(nearest[:], dist[:, 0, :], dist[:, 1, :], ALU.min)
+            for n in range(2, NK):
+                nc.vector.tensor_tensor(nearest[:], nearest[:], dist[:, n, :], ALU.min)
+            gauss = soft.tile([P, NK, PIECE], F32, name="gauss")
+            for n in range(NK):
+                nc.vector.tensor_tensor(dist[:, n, :], dist[:, n, :], nearest[:], ALU.subtract)
+                nc.scalar.activation(gauss[:, n, :], dist[:, n, :], ACT.Exp, scale=-1.0)
+            total = soft.tile([P, PIECE], F32, name="total")
+            nc.vector.tensor_tensor(total[:], gauss[:, 0, :], gauss[:, 1, :], ALU.add)
+            for n in range(2, NK):
+                nc.vector.tensor_tensor(total[:], total[:], gauss[:, n, :], ALU.add)
+            log_total = soft.tile([P, PIECE], F32, name="log_total")
+            nc.scalar.activation(log_total[:], total[:], ACT.Ln)
+            inv_total = soft.tile([P, PIECE], F32, name="inv_total")
+            nc.scalar.activation(inv_total[:], log_total[:], ACT.Exp, scale=-1.0)
+            share = soft.tile([P, NK, PIECE], BF16, name="share")
+            ws = weights.tile([P, NK, PIECE], F32, name="ws")
+            for n in range(NK):
+                nc.vector.tensor_tensor(share[:, n, :], gauss[:, n, :], inv_total[:], ALU.mult)
+                for h in range(BANKS):
+                    cols = slice(h * BANK, (h + 1) * BANK)
+                    ws_bank = sums.tile([P, BANK], F32, name="ws_bank")
+                    nc.tensor.matmul(ws_bank[:], ones[:], share[:, n, cols], start=True, stop=True)
+                    nc.scalar.copy(ws[:, n, cols], ws_bank[:])
+            return ws
+
+        def convolve(piece, ws):
+            piece_offsets = offsets[:, piece * (PIECE // 16) : (piece + 1) * (PIECE // 16)]
+            for n in range(NK):
+                acc = [
+                    [accs.tile([P, BANK], F32, name="acc") for h in range(BANKS)] for o in range(O_BLOCKS)
+                ]
+                for b in range(D_BLOCKS):
+                    y = products.tile([P, PIECE], F32, name="y")
+                    nc.vector.tensor_tensor(y[:], x_blocks[b][:].indirect(piece_offsets), ws[:, n, :], ALU.mult)
+                    y_bf = products.tile([P, PIECE], BF16, name="y_bf")
+                    nc.scalar.copy(y_bf[:], y[:])
+                    for o in range(O_BLOCKS):
+                        first = n * OP + o * P
+                        for h in range(BANKS):
+                            nc.tensor.matmul(
+                                acc[o][h][:],
+                                w_sb[:, b, first : first + P],
+                                y_bf[:, h * BANK : (h + 1) * BANK],
+                                start=(b == 0),
+                                stop=(b == D_BLOCKS - 1),
+                            )
+                for o in range(O_BLOCKS):
+                    first = n * OP + o * P
+                    staged = staging.tile([P, PIECE], F32, name="staged")
+                    for h in range(BANKS):
+                        nc.scalar.copy(staged[:, h * BANK : (h + 1) * BANK], acc[o][h][:])
+                    nc.sync.dma_start(out[first : first + P, piece * PIECE : (piece + 1) * PIECE], staged[:])
+
+        pieces = N // PIECE
+        ws_next = relation_weights(0)
+        for piece in range(pieces):
+            ws_now = ws_next
+            if piece + 1 < pieces:
+                ws_next = relation_weights(piece + 1)
+            convolve(piece, ws_now)

@@ -57,7 +57,7 @@ def tile_visualconvolution_b_kernel(tc, x, rel, mean_rel, prec_rel, w, offs, out
         shift = held.tile([P, NK], F32, name="shift")
         nc.vector.tensor_tensor(shift[:], neg_mean[:], slope[:], ALU.mult)
 
-        def relation_weights(piece):
+        def relation_weights(piece, elementwise):
             rel_piece = rel_sb[:, piece * PIECE : (piece + 1) * PIECE]
             dist = soft.tile([P, NK, PIECE], F32, name="dist")
             for n in range(NK):
@@ -70,12 +70,12 @@ def tile_visualconvolution_b_kernel(tc, x, rel, mean_rel, prec_rel, w, offs, out
                 nc.vector.tensor_tensor(nearest[:], nearest[:], dist[:, n, :], ALU.min)
             gauss = soft.tile([P, NK, PIECE], F32, name="gauss")
             for n in range(NK):
-                nc.vector.tensor_tensor(dist[:, n, :], dist[:, n, :], nearest[:], ALU.subtract)
+                elementwise.tensor_tensor(dist[:, n, :], dist[:, n, :], nearest[:], ALU.subtract)
                 nc.scalar.activation(gauss[:, n, :], dist[:, n, :], ACT.Exp, scale=-1.0)
             total = soft.tile([P, PIECE], F32, name="total")
-            nc.vector.tensor_tensor(total[:], gauss[:, 0, :], gauss[:, 1, :], ALU.add)
+            elementwise.tensor_tensor(total[:], gauss[:, 0, :], gauss[:, 1, :], ALU.add)
             for n in range(2, NK):
-                nc.vector.tensor_tensor(total[:], total[:], gauss[:, n, :], ALU.add)
+                elementwise.tensor_tensor(total[:], total[:], gauss[:, n, :], ALU.add)
             log_total = soft.tile([P, PIECE], F32, name="log_total")
             nc.scalar.activation(log_total[:], total[:], ACT.Ln)
             inv_total = soft.tile([P, PIECE], F32, name="inv_total")
@@ -83,7 +83,7 @@ def tile_visualconvolution_b_kernel(tc, x, rel, mean_rel, prec_rel, w, offs, out
             share = soft.tile([P, NK, PIECE], BF16, name="share")
             ws = weights.tile([P, NK, PIECE], F32, name="ws")
             for n in range(NK):
-                nc.vector.tensor_tensor(share[:, n, :], gauss[:, n, :], inv_total[:], ALU.mult)
+                elementwise.tensor_tensor(share[:, n, :], gauss[:, n, :], inv_total[:], ALU.mult)
                 for h in range(BANKS):
                     cols = slice(h * BANK, (h + 1) * BANK)
                     ws_bank = sums.tile([P, BANK], F32, name="ws_bank")
@@ -120,9 +120,9 @@ def tile_visualconvolution_b_kernel(tc, x, rel, mean_rel, prec_rel, w, offs, out
                     nc.sync.dma_start(out[first : first + P, piece * PIECE : (piece + 1) * PIECE], staged[:])
 
         pieces = N // PIECE
-        ws_next = relation_weights(0)
+        ws_next = relation_weights(0, nc.vector)
         for piece in range(pieces):
             ws_now = ws_next
             if piece + 1 < pieces:
-                ws_next = relation_weights(piece + 1)
+                ws_next = relation_weights(piece + 1, nc.gpsimd)
             convolve(piece, ws_now)

@@ -13,9 +13,9 @@ D, S, N = 1024, 2048, 3072
 NK, OP = 4, 256
 D_BLOCKS = D // P
 O_BLOCKS = OP // P
-PIECE = 1024
-BANK = 512
-BANKS = PIECE // BANK
+PIECE = 512
+PIECES = N // PIECE
+AHEAD = 2
 
 FLOPS = 2 * D * NK * OP * N
 
@@ -24,12 +24,12 @@ def tile_visualconvolution_b_kernel(tc, x, rel, mean_rel, prec_rel, w, offs, out
     nc = tc.nc
     with (
         tc.tile_pool(name="held", bufs=1) as held,
-        tc.tile_pool(name="weights", bufs=2) as weights,
-        tc.tile_pool(name="soft", bufs=1) as soft,
-        tc.tile_pool(name="products", bufs=4) as products,
-        tc.tile_pool(name="staging", bufs=3) as staging,
+        tc.tile_pool(name="weights", bufs=AHEAD + 1) as weights,
+        tc.tile_pool(name="soft", bufs=2) as soft,
+        tc.tile_pool(name="products", bufs=6) as products,
+        tc.tile_pool(name="staging", bufs=4) as staging,
         tc.psum_pool(name="sums", bufs=2) as sums,
-        tc.psum_pool(name="accs", bufs=6) as accs,
+        tc.psum_pool(name="accs", bufs=3 * O_BLOCKS) as accs,
     ):
         offsets = held.tile([P, N // 16], U16, name="offsets")
         nc.sync.dma_start(offsets[:], offs)
@@ -44,7 +44,9 @@ def tile_visualconvolution_b_kernel(tc, x, rel, mean_rel, prec_rel, w, offs, out
         for b in range(D_BLOCKS):
             nc.sync.dma_start(x_blocks[b][:], x[b * P : (b + 1) * P, :])
             nc.sync.dma_start(w_sb[:, b, :], w[b * P : (b + 1) * P, :])
-        nc.sync.dma_start(rel_sb[:, PIECE:N], rel[:, PIECE:N])
+            if b + 1 < PIECES:
+                later = slice((b + 1) * PIECE, (b + 2) * PIECE)
+                nc.sync.dma_start(rel_sb[:, later], rel[:, later])
 
         ones = held.tile([P, P], BF16, name="ones")
         nc.gpsimd.memset(ones[:], 1.0)
@@ -57,7 +59,7 @@ def tile_visualconvolution_b_kernel(tc, x, rel, mean_rel, prec_rel, w, offs, out
         shift = held.tile([P, NK], F32, name="shift")
         nc.vector.tensor_tensor(shift[:], neg_mean[:], slope[:], ALU.mult)
 
-        def relation_weights(piece, elementwise):
+        def relation_weights(piece):
             rel_piece = rel_sb[:, piece * PIECE : (piece + 1) * PIECE]
             dist = soft.tile([P, NK, PIECE], F32, name="dist")
             for n in range(NK):
@@ -70,12 +72,12 @@ def tile_visualconvolution_b_kernel(tc, x, rel, mean_rel, prec_rel, w, offs, out
                 nc.vector.tensor_tensor(nearest[:], nearest[:], dist[:, n, :], ALU.min)
             gauss = soft.tile([P, NK, PIECE], F32, name="gauss")
             for n in range(NK):
-                elementwise.tensor_tensor(dist[:, n, :], dist[:, n, :], nearest[:], ALU.subtract)
+                nc.vector.tensor_tensor(dist[:, n, :], dist[:, n, :], nearest[:], ALU.subtract)
                 nc.scalar.activation(gauss[:, n, :], dist[:, n, :], ACT.Exp, scale=-1.0)
             total = soft.tile([P, PIECE], F32, name="total")
-            elementwise.tensor_tensor(total[:], gauss[:, 0, :], gauss[:, 1, :], ALU.add)
+            nc.vector.tensor_tensor(total[:], gauss[:, 0, :], gauss[:, 1, :], ALU.add)
             for n in range(2, NK):
-                elementwise.tensor_tensor(total[:], total[:], gauss[:, n, :], ALU.add)
+                nc.vector.tensor_tensor(total[:], total[:], gauss[:, n, :], ALU.add)
             log_total = soft.tile([P, PIECE], F32, name="log_total")
             nc.scalar.activation(log_total[:], total[:], ACT.Ln)
             inv_total = soft.tile([P, PIECE], F32, name="inv_total")
@@ -83,20 +85,16 @@ def tile_visualconvolution_b_kernel(tc, x, rel, mean_rel, prec_rel, w, offs, out
             share = soft.tile([P, NK, PIECE], BF16, name="share")
             ws = weights.tile([P, NK, PIECE], F32, name="ws")
             for n in range(NK):
-                elementwise.tensor_tensor(share[:, n, :], gauss[:, n, :], inv_total[:], ALU.mult)
-                for h in range(BANKS):
-                    cols = slice(h * BANK, (h + 1) * BANK)
-                    ws_bank = sums.tile([P, BANK], F32, name="ws_bank")
-                    nc.tensor.matmul(ws_bank[:], ones[:], share[:, n, cols], start=True, stop=True)
-                    nc.scalar.copy(ws[:, n, cols], ws_bank[:])
+                nc.vector.tensor_tensor(share[:, n, :], gauss[:, n, :], inv_total[:], ALU.mult)
+                ws_bank = sums.tile([P, PIECE], F32, name="ws_bank")
+                nc.tensor.matmul(ws_bank[:], ones[:], share[:, n, :], start=True, stop=True)
+                nc.scalar.copy(ws[:, n, :], ws_bank[:])
             return ws
 
         def convolve(piece, ws):
             piece_offsets = offsets[:, piece * (PIECE // 16) : (piece + 1) * (PIECE // 16)]
             for n in range(NK):
-                acc = [
-                    [accs.tile([P, BANK], F32, name="acc") for h in range(BANKS)] for o in range(O_BLOCKS)
-                ]
+                acc = [accs.tile([P, PIECE], F32, name="acc") for o in range(O_BLOCKS)]
                 for b in range(D_BLOCKS):
                     y = products.tile([P, PIECE], F32, name="y")
                     nc.vector.tensor_tensor(y[:], x_blocks[b][:].indirect(piece_offsets), ws[:, n, :], ALU.mult)
@@ -104,25 +102,17 @@ def tile_visualconvolution_b_kernel(tc, x, rel, mean_rel, prec_rel, w, offs, out
                     nc.scalar.copy(y_bf[:], y[:])
                     for o in range(O_BLOCKS):
                         first = n * OP + o * P
-                        for h in range(BANKS):
-                            nc.tensor.matmul(
-                                acc[o][h][:],
-                                w_sb[:, b, first : first + P],
-                                y_bf[:, h * BANK : (h + 1) * BANK],
-                                start=(b == 0),
-                                stop=(b == D_BLOCKS - 1),
-                            )
+                        nc.tensor.matmul(
+                            acc[o][:], w_sb[:, b, first : first + P], y_bf[:], start=(b == 0), stop=(b == D_BLOCKS - 1)
+                        )
                 for o in range(O_BLOCKS):
                     first = n * OP + o * P
                     staged = staging.tile([P, PIECE], F32, name="staged")
-                    for h in range(BANKS):
-                        nc.scalar.copy(staged[:, h * BANK : (h + 1) * BANK], acc[o][h][:])
+                    nc.scalar.copy(staged[:], acc[o][:])
                     nc.sync.dma_start(out[first : first + P, piece * PIECE : (piece + 1) * PIECE], staged[:])
 
-        pieces = N // PIECE
-        ws_next = relation_weights(0, nc.vector)
-        for piece in range(pieces):
-            ws_now = ws_next
-            if piece + 1 < pieces:
-                ws_next = relation_weights(piece + 1, nc.gpsimd)
-            convolve(piece, ws_now)
+        ws_of = [relation_weights(piece) for piece in range(AHEAD)]
+        for piece in range(PIECES):
+            if piece + AHEAD < PIECES:
+                ws_of.append(relation_weights(piece + AHEAD))
+            convolve(piece, ws_of[piece])

@@ -1,6 +1,7 @@
 import math
 
 import concourse.mybir as mybir
+from concourse.masks import make_identity
 
 F32 = mybir.dt.float32
 BF16 = mybir.dt.bfloat16
@@ -13,23 +14,29 @@ D, S, N = 1024, 2048, 3072
 NK, OP = 4, 256
 D_BLOCKS = D // P
 O_BLOCKS = OP // P
-PIECE = 512
-PIECES = N // PIECE
-AHEAD = 2
+BANK = 512
+PIECES = (256, 512, 1024, 1024, 256)
+assert sum(PIECES) == N and all(width % 32 == 0 for width in PIECES)
 
 FLOPS = 2 * D * NK * OP * N
 
 
+def bank_chunks(width):
+    return [(lo, min(lo + BANK, width)) for lo in range(0, width, BANK)]
+
+
 def tile_visualconvolution_b_kernel(tc, x, rel, mean_rel, prec_rel, w, offs, out):
     nc = tc.nc
+    starts = [sum(PIECES[:i]) for i in range(len(PIECES))]
     with (
         tc.tile_pool(name="held", bufs=1) as held,
-        tc.tile_pool(name="weights", bufs=AHEAD + 1) as weights,
-        tc.tile_pool(name="soft", bufs=2) as soft,
+        tc.tile_pool(name="weights", bufs=2) as weights,
+        tc.tile_pool(name="soft", bufs=1) as soft,
         tc.tile_pool(name="products", bufs=6) as products,
-        tc.tile_pool(name="staging", bufs=4) as staging,
-        tc.psum_pool(name="sums", bufs=2) as sums,
-        tc.psum_pool(name="accs", bufs=3 * O_BLOCKS) as accs,
+        tc.tile_pool(name="rounded", bufs=10) as rounded,
+        tc.tile_pool(name="staging", bufs=3) as staging,
+        tc.psum_pool(name="banks", bufs=4) as banks,
+        tc.psum_pool(name="accs", bufs=4) as accs,
     ):
         offsets = held.tile([P, N // 16], U16, name="offsets")
         nc.sync.dma_start(offsets[:], offs)
@@ -38,18 +45,26 @@ def tile_visualconvolution_b_kernel(tc, x, rel, mean_rel, prec_rel, w, offs, out
         width_all = held.tile([P, NK], F32, name="width_all")
         nc.sync.dma_start(width_all[:], prec_rel.broadcast_to([P, NK]))
         rel_sb = held.tile([P, N], F32, name="rel_sb")
-        nc.sync.dma_start(rel_sb[:, 0:PIECE], rel[:, 0:PIECE])
         x_blocks = [held.tile([P, S], F32, name=f"x{b}") for b in range(D_BLOCKS)]
         w_sb = held.tile([P, D_BLOCKS, NK * OP], BF16, name="w_sb")
+        nc.sync.dma_start(rel_sb[:, 0 : PIECES[0]], rel[:, 0 : PIECES[0]])
         for b in range(D_BLOCKS):
             nc.sync.dma_start(x_blocks[b][:], x[b * P : (b + 1) * P, :])
             nc.sync.dma_start(w_sb[:, b, :], w[b * P : (b + 1) * P, :])
-            if b + 1 < PIECES:
-                later = slice((b + 1) * PIECE, (b + 2) * PIECE)
+            if b + 1 < len(PIECES):
+                later = slice(starts[b + 1], starts[b + 1] + PIECES[b + 1])
                 nc.sync.dma_start(rel_sb[:, later], rel[:, later])
 
         ones = held.tile([P, P], BF16, name="ones")
         nc.gpsimd.memset(ones[:], 1.0)
+        warm = held.tile([P, 1], F32, name="warm")
+        nc.scalar.activation(warm[:], ones[:, 0:1], ACT.Exp)
+        identity = held.tile([P, P], F32, name="identity")
+        make_identity(nc, identity[:])
+        minus_identity = held.tile([P, P], F32, name="minus_identity")
+        nc.vector.tensor_scalar_mul(minus_identity[:], identity[:], -1.0)
+        identity_bf = held.tile([P, P], BF16, name="identity_bf")
+        nc.vector.tensor_copy(identity_bf[:], identity[:])
         inv_width = held.tile([P, NK], F32, name="inv_width")
         nc.vector.reciprocal(inv_width[:], width_all[:])
         slope = held.tile([P, NK], F32, name="slope")
@@ -59,60 +74,87 @@ def tile_visualconvolution_b_kernel(tc, x, rel, mean_rel, prec_rel, w, offs, out
         shift = held.tile([P, NK], F32, name="shift")
         nc.vector.tensor_tensor(shift[:], neg_mean[:], slope[:], ALU.mult)
 
-        def relation_weights(piece):
-            rel_piece = rel_sb[:, piece * PIECE : (piece + 1) * PIECE]
-            dist = soft.tile([P, NK, PIECE], F32, name="dist")
+        def relation_weights(start, width, vector_is_idle):
+            chunks = bank_chunks(width)
+            dist = soft.tile([P, NK, width], F32, name="dist")
             for n in range(NK):
                 nc.scalar.activation(
-                    dist[:, n, :], rel_piece, ACT.Square, bias=shift[:, n : n + 1], scale=slope[:, n : n + 1]
+                    dist[:, n, :],
+                    rel_sb[:, start : start + width],
+                    ACT.Square,
+                    bias=shift[:, n : n + 1],
+                    scale=slope[:, n : n + 1],
                 )
-            nearest = soft.tile([P, PIECE], F32, name="nearest")
+            nearest = soft.tile([P, width], F32, name="nearest")
             nc.vector.tensor_tensor(nearest[:], dist[:, 0, :], dist[:, 1, :], ALU.min)
-            for n in range(2, NK):
-                nc.vector.tensor_tensor(nearest[:], nearest[:], dist[:, n, :], ALU.min)
-            gauss = soft.tile([P, NK, PIECE], F32, name="gauss")
-            for n in range(NK):
-                nc.vector.tensor_tensor(dist[:, n, :], dist[:, n, :], nearest[:], ALU.subtract)
-                nc.scalar.activation(gauss[:, n, :], dist[:, n, :], ACT.Exp, scale=-1.0)
-            total = soft.tile([P, PIECE], F32, name="total")
-            nc.vector.tensor_tensor(total[:], gauss[:, 0, :], gauss[:, 1, :], ALU.add)
-            for n in range(2, NK):
-                nc.vector.tensor_tensor(total[:], total[:], gauss[:, n, :], ALU.add)
-            log_total = soft.tile([P, PIECE], F32, name="log_total")
-            nc.scalar.activation(log_total[:], total[:], ACT.Ln)
-            inv_total = soft.tile([P, PIECE], F32, name="inv_total")
+            nc.vector.tensor_tensor(nearest[:], nearest[:], dist[:, 2, :], ALU.min)
+            level = soft.tile([P, width], BF16, name="level")
+            nc.vector.tensor_tensor(level[:], nearest[:], dist[:, 3, :], ALU.min)
+            gauss = soft.tile([P, NK, width], F32, name="gauss")
+            log_total = soft.tile([P, width], F32, name="log_total")
+            if vector_is_idle:
+                for n in range(NK):
+                    nc.vector.tensor_tensor(dist[:, n, :], level[:], dist[:, n, :], ALU.subtract)
+                    nc.scalar.activation(gauss[:, n, :], dist[:, n, :], ACT.Exp)
+                total_sb = soft.tile([P, width], F32, name="total_sb")
+                nc.vector.tensor_tensor(total_sb[:], gauss[:, 0, :], gauss[:, 1, :], ALU.add)
+                for n in range(2, NK):
+                    nc.vector.tensor_tensor(total_sb[:], total_sb[:], gauss[:, n, :], ALU.add)
+                nc.scalar.activation(log_total[:], total_sb[:], ACT.Ln)
+            else:
+                for lo, hi in chunks:
+                    for n in range(NK):
+                        exponent = banks.tile([P, hi - lo], F32, name="exponent", tag="bank")
+                        nc.tensor.matmul(exponent[:], minus_identity[:], dist[:, n, lo:hi], start=True, stop=False)
+                        nc.tensor.matmul(exponent[:], identity_bf[:], level[:, lo:hi], start=False, stop=True)
+                        nc.scalar.activation(gauss[:, n, lo:hi], exponent[:], ACT.Exp)
+                for lo, hi in chunks:
+                    total = banks.tile([P, hi - lo], F32, name="total", tag="bank")
+                    for n in range(NK):
+                        nc.tensor.matmul(total[:], identity[:], gauss[:, n, lo:hi], start=(n == 0), stop=(n == NK - 1))
+                    nc.scalar.activation(log_total[:, lo:hi], total[:], ACT.Ln)
+            inv_total = soft.tile([P, width], F32, name="inv_total")
             nc.scalar.activation(inv_total[:], log_total[:], ACT.Exp, scale=-1.0)
-            share = soft.tile([P, NK, PIECE], BF16, name="share")
-            ws = weights.tile([P, NK, PIECE], F32, name="ws")
+            share = soft.tile([P, NK, width], BF16, name="share")
+            ws = weights.tile([P, NK, width], F32, name="ws")
             for n in range(NK):
                 nc.vector.tensor_tensor(share[:, n, :], gauss[:, n, :], inv_total[:], ALU.mult)
-                ws_bank = sums.tile([P, PIECE], F32, name="ws_bank")
-                nc.tensor.matmul(ws_bank[:], ones[:], share[:, n, :], start=True, stop=True)
-                nc.scalar.copy(ws[:, n, :], ws_bank[:])
+                for lo, hi in chunks:
+                    ws_bank = banks.tile([P, hi - lo], F32, name="ws_bank", tag="bank")
+                    nc.tensor.matmul(ws_bank[:], ones[:], share[:, n, lo:hi], start=True, stop=True)
+                    nc.scalar.copy(ws[:, n, lo:hi], ws_bank[:])
             return ws
 
-        def convolve(piece, ws):
-            piece_offsets = offsets[:, piece * (PIECE // 16) : (piece + 1) * (PIECE // 16)]
+        def convolve(start, width, ws):
+            chunks = bank_chunks(width)
+            piece_offsets = offsets[:, start // 16 : (start + width) // 16]
             for n in range(NK):
-                acc = [accs.tile([P, PIECE], F32, name="acc") for o in range(O_BLOCKS)]
+                acc = [[accs.tile([P, hi - lo], F32, name="acc") for lo, hi in chunks] for o in range(O_BLOCKS)]
                 for b in range(D_BLOCKS):
-                    y = products.tile([P, PIECE], F32, name="y")
+                    y = products.tile([P, width], F32, name="y")
                     nc.vector.tensor_tensor(y[:], x_blocks[b][:].indirect(piece_offsets), ws[:, n, :], ALU.mult)
-                    y_bf = products.tile([P, PIECE], BF16, name="y_bf")
+                    y_bf = rounded.tile([P, width], BF16, name="y_bf")
                     nc.scalar.copy(y_bf[:], y[:])
                     for o in range(O_BLOCKS):
                         first = n * OP + o * P
-                        nc.tensor.matmul(
-                            acc[o][:], w_sb[:, b, first : first + P], y_bf[:], start=(b == 0), stop=(b == D_BLOCKS - 1)
-                        )
+                        for c, (lo, hi) in enumerate(chunks):
+                            nc.tensor.matmul(
+                                acc[o][c][:],
+                                w_sb[:, b, first : first + P],
+                                y_bf[:, lo:hi],
+                                start=(b == 0),
+                                stop=(b == D_BLOCKS - 1),
+                            )
                 for o in range(O_BLOCKS):
                     first = n * OP + o * P
-                    staged = staging.tile([P, PIECE], F32, name="staged")
-                    nc.scalar.copy(staged[:], acc[o][:])
-                    nc.sync.dma_start(out[first : first + P, piece * PIECE : (piece + 1) * PIECE], staged[:])
+                    staged = staging.tile([P, width], F32, name="staged")
+                    for c, (lo, hi) in enumerate(chunks):
+                        nc.scalar.copy(staged[:, lo:hi], acc[o][c][:])
+                    nc.sync.dma_start(out[first : first + P, start : start + width], staged[:])
 
-        ws_of = [relation_weights(piece) for piece in range(AHEAD)]
-        for piece in range(PIECES):
-            if piece + AHEAD < PIECES:
-                ws_of.append(relation_weights(piece + AHEAD))
-            convolve(piece, ws_of[piece])
+        ws_next = relation_weights(starts[0], PIECES[0], vector_is_idle=True)
+        for i, width in enumerate(PIECES):
+            ws_now = ws_next
+            if i + 1 < len(PIECES):
+                ws_next = relation_weights(starts[i + 1], PIECES[i + 1], vector_is_idle=False)
+            convolve(starts[i], width, ws_now)

@@ -15,7 +15,7 @@ NK, OP = 4, 256
 D_BLOCKS = D // P
 O_BLOCKS = OP // P
 BANK = 512
-PIECES = (256, 512, 1024, 1024, 256)
+PIECES = (512, 1024, 1024, 512)
 assert sum(PIECES) == N and all(width % 32 == 0 for width in PIECES)
 
 FLOPS = 2 * D * NK * OP * N

@@ -38,16 +38,16 @@ def tile_visualconvolution_b_kernel(tc, x, rel, mean_rel, prec_rel, w, offs, out
         tc.psum_pool(name="banks", bufs=4) as banks,
         tc.psum_pool(name="accs", bufs=4) as accs,
     ):
+        mean_all = held.tile([P, NK], F32, name="mean_all")
+        nc.scalar.dma_start(mean_all[:], mean_rel.broadcast_to([P, NK]))
+        width_all = held.tile([P, NK], F32, name="width_all")
+        nc.scalar.dma_start(width_all[:], prec_rel.broadcast_to([P, NK]))
+        rel_sb = held.tile([P, N], F32, name="rel_sb")
+        nc.sync.dma_start(rel_sb[:, 0 : PIECES[0]], rel[:, 0 : PIECES[0]])
         offsets = held.tile([P, N // 16], U16, name="offsets")
         nc.sync.dma_start(offsets[:], offs)
-        mean_all = held.tile([P, NK], F32, name="mean_all")
-        nc.sync.dma_start(mean_all[:], mean_rel.broadcast_to([P, NK]))
-        width_all = held.tile([P, NK], F32, name="width_all")
-        nc.sync.dma_start(width_all[:], prec_rel.broadcast_to([P, NK]))
-        rel_sb = held.tile([P, N], F32, name="rel_sb")
         x_blocks = [held.tile([P, S], F32, name=f"x{b}") for b in range(D_BLOCKS)]
         w_sb = held.tile([P, D_BLOCKS, NK * OP], BF16, name="w_sb")
-        nc.sync.dma_start(rel_sb[:, 0 : PIECES[0]], rel[:, 0 : PIECES[0]])
         for b in range(D_BLOCKS):
             nc.sync.dma_start(x_blocks[b][:], x[b * P : (b + 1) * P, :])
             nc.sync.dma_start(w_sb[:, b, :], w[b * P : (b + 1) * P, :])
@@ -91,7 +91,7 @@ def tile_visualconvolution_b_kernel(tc, x, rel, mean_rel, prec_rel, w, offs, out
             level = soft.tile([P, width], BF16, name="level")
             nc.vector.tensor_tensor(level[:], nearest[:], dist[:, 3, :], ALU.min)
             gauss = soft.tile([P, NK, width], F32, name="gauss")
-            log_total = soft.tile([P, width], F32, name="log_total")
+            inv_total = soft.tile([P, width], F32, name="inv_total")
             if vector_is_idle:
                 for n in range(NK):
                     nc.vector.tensor_tensor(dist[:, n, :], level[:], dist[:, n, :], ALU.subtract)
@@ -100,7 +100,7 @@ def tile_visualconvolution_b_kernel(tc, x, rel, mean_rel, prec_rel, w, offs, out
                 nc.vector.tensor_tensor(total_sb[:], gauss[:, 0, :], gauss[:, 1, :], ALU.add)
                 for n in range(2, NK):
                     nc.vector.tensor_tensor(total_sb[:], total_sb[:], gauss[:, n, :], ALU.add)
-                nc.scalar.activation(log_total[:], total_sb[:], ACT.Ln)
+                nc.vector.reciprocal(inv_total[:], total_sb[:])
             else:
                 for lo, hi in chunks:
                     for n in range(NK):
@@ -108,13 +108,13 @@ def tile_visualconvolution_b_kernel(tc, x, rel, mean_rel, prec_rel, w, offs, out
                         nc.tensor.matmul(exponent[:], minus_identity[:], dist[:, n, lo:hi], start=True, stop=False)
                         nc.tensor.matmul(exponent[:], identity_bf[:], level[:, lo:hi], start=False, stop=True)
                         nc.scalar.activation(gauss[:, n, lo:hi], exponent[:], ACT.Exp)
+                log_total = soft.tile([P, width], F32, name="log_total")
                 for lo, hi in chunks:
                     total = banks.tile([P, hi - lo], F32, name="total", tag="bank")
                     for n in range(NK):
                         nc.tensor.matmul(total[:], identity[:], gauss[:, n, lo:hi], start=(n == 0), stop=(n == NK - 1))
                     nc.scalar.activation(log_total[:, lo:hi], total[:], ACT.Ln)
-            inv_total = soft.tile([P, width], F32, name="inv_total")
-            nc.scalar.activation(inv_total[:], log_total[:], ACT.Exp, scale=-1.0)
+                nc.scalar.activation(inv_total[:], log_total[:], ACT.Exp, scale=-1.0)
             share = soft.tile([P, NK, width], BF16, name="share")
             ws = weights.tile([P, NK, width], F32, name="ws")
             for n in range(NK):

@@ -15,6 +15,7 @@ NK, OP = 4, 256
 D_BLOCKS = D // P
 O_BLOCKS = OP // P
 BANK = 512
+SOFTEN = 16.0
 PIECES = (512, 1024, 1024, 512)
 assert sum(PIECES) == N and all(width % 32 == 0 for width in PIECES)
 
@@ -65,6 +66,8 @@ def tile_visualconvolution_b_kernel(tc, x, rel, mean_rel, prec_rel, w, offs, out
         nc.vector.tensor_scalar_mul(minus_identity[:], identity[:], -1.0)
         identity_bf = held.tile([P, P], BF16, name="identity_bf")
         nc.vector.tensor_copy(identity_bf[:], identity[:])
+        minus_soften_bf = held.tile([P, P], BF16, name="minus_soften_bf")
+        nc.vector.tensor_scalar_mul(minus_soften_bf[:], identity[:], -SOFTEN)
         inv_width = held.tile([P, NK], F32, name="inv_width")
         nc.vector.reciprocal(inv_width[:], width_all[:])
         slope = held.tile([P, NK], F32, name="slope")
@@ -74,7 +77,7 @@ def tile_visualconvolution_b_kernel(tc, x, rel, mean_rel, prec_rel, w, offs, out
         shift = held.tile([P, NK], F32, name="shift")
         nc.vector.tensor_tensor(shift[:], neg_mean[:], slope[:], ALU.mult)
 
-        def relation_weights(start, width, vector_is_idle):
+        def relation_weights(start, width, vector_does):
             chunks = bank_chunks(width)
             dist = soft.tile([P, NK, width], F32, name="dist")
             for n in range(NK):
@@ -85,14 +88,26 @@ def tile_visualconvolution_b_kernel(tc, x, rel, mean_rel, prec_rel, w, offs, out
                     bias=shift[:, n : n + 1],
                     scale=slope[:, n : n + 1],
                 )
-            nearest = soft.tile([P, width], F32, name="nearest")
-            nc.vector.tensor_tensor(nearest[:], dist[:, 0, :], dist[:, 1, :], ALU.min)
-            nc.vector.tensor_tensor(nearest[:], nearest[:], dist[:, 2, :], ALU.min)
             level = soft.tile([P, width], BF16, name="level")
-            nc.vector.tensor_tensor(level[:], nearest[:], dist[:, 3, :], ALU.min)
+            if vector_does == "none":
+                level_factor = minus_soften_bf
+                flat = soft.tile([P, NK, width], BF16, name="flat", tag="share")
+                for n in range(NK):
+                    nc.scalar.activation(flat[:, n, :], dist[:, n, :], ACT.Exp, scale=-1.0 / SOFTEN)
+                for lo, hi in chunks:
+                    flat_total = banks.tile([P, hi - lo], F32, name="flat_total", tag="bank")
+                    for n in range(NK):
+                        nc.tensor.matmul(flat_total[:], identity_bf[:], flat[:, n, lo:hi], start=(n == 0), stop=(n == NK - 1))
+                    nc.scalar.activation(level[:, lo:hi], flat_total[:], ACT.Ln)
+            else:
+                level_factor = identity_bf
+                nearest = soft.tile([P, width], F32, name="nearest")
+                nc.vector.tensor_tensor(nearest[:], dist[:, 0, :], dist[:, 1, :], ALU.min)
+                nc.vector.tensor_tensor(nearest[:], nearest[:], dist[:, 2, :], ALU.min)
+                nc.vector.tensor_tensor(level[:], nearest[:], dist[:, 3, :], ALU.min)
             gauss = soft.tile([P, NK, width], F32, name="gauss")
-            inv_total = soft.tile([P, width], F32, name="inv_total")
-            if vector_is_idle:
+            share = soft.tile([P, NK, width], BF16, name="share")
+            if vector_does == "all":
                 for n in range(NK):
                     nc.vector.tensor_tensor(dist[:, n, :], level[:], dist[:, n, :], ALU.subtract)
                     nc.scalar.activation(gauss[:, n, :], dist[:, n, :], ACT.Exp)
@@ -100,13 +115,14 @@ def tile_visualconvolution_b_kernel(tc, x, rel, mean_rel, prec_rel, w, offs, out
                 nc.vector.tensor_tensor(total_sb[:], gauss[:, 0, :], gauss[:, 1, :], ALU.add)
                 for n in range(2, NK):
                     nc.vector.tensor_tensor(total_sb[:], total_sb[:], gauss[:, n, :], ALU.add)
+                inv_total = soft.tile([P, width], F32, name="inv_total")
                 nc.vector.reciprocal(inv_total[:], total_sb[:])
             else:
                 for lo, hi in chunks:
                     for n in range(NK):
                         exponent = banks.tile([P, hi - lo], F32, name="exponent", tag="bank")
                         nc.tensor.matmul(exponent[:], minus_identity[:], dist[:, n, lo:hi], start=True, stop=False)
-                        nc.tensor.matmul(exponent[:], identity_bf[:], level[:, lo:hi], start=False, stop=True)
+                        nc.tensor.matmul(exponent[:], level_factor[:], level[:, lo:hi], start=False, stop=True)
                         nc.scalar.activation(gauss[:, n, lo:hi], exponent[:], ACT.Exp)
                 log_total = soft.tile([P, width], F32, name="log_total")
                 for lo, hi in chunks:
@@ -114,11 +130,21 @@ def tile_visualconvolution_b_kernel(tc, x, rel, mean_rel, prec_rel, w, offs, out
                     for n in range(NK):
                         nc.tensor.matmul(total[:], identity[:], gauss[:, n, lo:hi], start=(n == 0), stop=(n == NK - 1))
                     nc.scalar.activation(log_total[:, lo:hi], total[:], ACT.Ln)
-                nc.scalar.activation(inv_total[:], log_total[:], ACT.Exp, scale=-1.0)
-            share = soft.tile([P, NK, width], BF16, name="share")
+                if vector_does == "some":
+                    inv_total = soft.tile([P, width], F32, name="inv_total")
+                    nc.scalar.activation(inv_total[:], log_total[:], ACT.Exp, scale=-1.0)
+            for n in range(NK):
+                if vector_does == "none":
+                    for lo, hi in chunks:
+                        exponent = banks.tile([P, hi - lo], F32, name="exponent", tag="bank")
+                        nc.tensor.matmul(exponent[:], minus_identity[:], dist[:, n, lo:hi], start=True, stop=False)
+                        nc.tensor.matmul(exponent[:], level_factor[:], level[:, lo:hi], start=False, stop=False)
+                        nc.tensor.matmul(exponent[:], minus_identity[:], log_total[:, lo:hi], start=False, stop=True)
+                        nc.scalar.activation(share[:, n, lo:hi], exponent[:], ACT.Exp)
+                else:
+                    nc.vector.tensor_tensor(share[:, n, :], gauss[:, n, :], inv_total[:], ALU.mult)
             ws = weights.tile([P, NK, width], F32, name="ws")
             for n in range(NK):
-                nc.vector.tensor_tensor(share[:, n, :], gauss[:, n, :], inv_total[:], ALU.mult)
                 for lo, hi in chunks:
                     ws_bank = banks.tile([P, hi - lo], F32, name="ws_bank", tag="bank")
                     nc.tensor.matmul(ws_bank[:], ones[:], share[:, n, lo:hi], start=True, stop=True)
@@ -152,9 +178,10 @@ def tile_visualconvolution_b_kernel(tc, x, rel, mean_rel, prec_rel, w, offs, out
                         nc.scalar.copy(staged[:, lo:hi], acc[o][c][:])
                     nc.sync.dma_start(out[first : first + P, start : start + width], staged[:])
 
-        ws_next = relation_weights(starts[0], PIECES[0], vector_is_idle=True)
+        ws_next = relation_weights(starts[0], PIECES[0], vector_does="all")
         for i, width in enumerate(PIECES):
             ws_now = ws_next
             if i + 1 < len(PIECES):
-                ws_next = relation_weights(starts[i + 1], PIECES[i + 1], vector_is_idle=False)
+                vector_does = "none" if i + 1 == len(PIECES) - 1 else "some"
+                ws_next = relation_weights(starts[i + 1], PIECES[i + 1], vector_does)
             convolve(starts[i], width, ws_now)

@@ -18,6 +18,7 @@ BANK = 512
 SOFTEN = 16.0
 PIECES = (512, 1024, 1024, 512)
 assert sum(PIECES) == N and all(width % 32 == 0 for width in PIECES)
+VECTOR_DOES = ("all", "some", "product", "none")
 
 FLOPS = 2 * D * NK * OP * N
 
@@ -89,7 +90,7 @@ def tile_visualconvolution_b_kernel(tc, x, rel, mean_rel, prec_rel, w, offs, out
                     scale=slope[:, n : n + 1],
                 )
             level = soft.tile([P, width], BF16, name="level")
-            if vector_does == "none":
+            if vector_does in ("product", "none"):
                 level_factor = minus_soften_bf
                 flat = soft.tile([P, NK, width], BF16, name="flat", tag="share")
                 for n in range(NK):
@@ -130,7 +131,7 @@ def tile_visualconvolution_b_kernel(tc, x, rel, mean_rel, prec_rel, w, offs, out
                     for n in range(NK):
                         nc.tensor.matmul(total[:], identity[:], gauss[:, n, lo:hi], start=(n == 0), stop=(n == NK - 1))
                     nc.scalar.activation(log_total[:, lo:hi], total[:], ACT.Ln)
-                if vector_does == "some":
+                if vector_does in ("some", "product"):
                     inv_total = soft.tile([P, width], F32, name="inv_total")
                     nc.scalar.activation(inv_total[:], log_total[:], ACT.Exp, scale=-1.0)
             for n in range(NK):
@@ -178,10 +179,9 @@ def tile_visualconvolution_b_kernel(tc, x, rel, mean_rel, prec_rel, w, offs, out
                         nc.scalar.copy(staged[:, lo:hi], acc[o][c][:])
                     nc.sync.dma_start(out[first : first + P, start : start + width], staged[:])
 
-        ws_next = relation_weights(starts[0], PIECES[0], vector_does="all")
+        ws_next = relation_weights(starts[0], PIECES[0], VECTOR_DOES[0])
         for i, width in enumerate(PIECES):
             ws_now = ws_next
             if i + 1 < len(PIECES):
-                vector_does = "none" if i + 1 == len(PIECES) - 1 else "some"
-                ws_next = relation_weights(starts[i + 1], PIECES[i + 1], vector_does)
+                ws_next = relation_weights(starts[i + 1], PIECES[i + 1], VECTOR_DOES[i + 1])
             convolve(starts[i], width, ws_now)

@@ -35,7 +35,7 @@ def tile_visualconvolution_b_kernel(tc, x, rel, mean_rel, prec_rel, w, offs, out
         tc.tile_pool(name="weights", bufs=2) as weights,
         tc.tile_pool(name="soft", bufs=1) as soft,
         tc.tile_pool(name="products", bufs=6) as products,
-        tc.tile_pool(name="rounded", bufs=10) as rounded,
+        tc.tile_pool(name="rounded", bufs=13) as rounded,
         tc.tile_pool(name="staging", bufs=3) as staging,
         tc.psum_pool(name="banks", bufs=4) as banks,
         tc.psum_pool(name="accs", bufs=4) as accs,
@@ -102,7 +102,7 @@ def tile_visualconvolution_b_kernel(tc, x, rel, mean_rel, prec_rel, w, offs, out
                     nc.scalar.activation(level[:, lo:hi], flat_total[:], ACT.Ln)
             else:
                 level_factor = identity_bf
-                nearest = soft.tile([P, width], F32, name="nearest")
+                nearest = soft.tile([P, width], F32, name="nearest", tag="row")
                 nc.vector.tensor_tensor(nearest[:], dist[:, 0, :], dist[:, 1, :], ALU.min)
                 nc.vector.tensor_tensor(nearest[:], nearest[:], dist[:, 2, :], ALU.min)
                 nc.vector.tensor_tensor(level[:], nearest[:], dist[:, 3, :], ALU.min)
@@ -112,7 +112,7 @@ def tile_visualconvolution_b_kernel(tc, x, rel, mean_rel, prec_rel, w, offs, out
                 for n in range(NK):
                     nc.vector.tensor_tensor(dist[:, n, :], level[:], dist[:, n, :], ALU.subtract)
                     nc.scalar.activation(gauss[:, n, :], dist[:, n, :], ACT.Exp)
-                total_sb = soft.tile([P, width], F32, name="total_sb")
+                total_sb = soft.tile([P, width], F32, name="total_sb", tag="row")
                 nc.vector.tensor_tensor(total_sb[:], gauss[:, 0, :], gauss[:, 1, :], ALU.add)
                 for n in range(2, NK):
                     nc.vector.tensor_tensor(total_sb[:], total_sb[:], gauss[:, n, :], ALU.add)
@@ -125,7 +125,7 @@ def tile_visualconvolution_b_kernel(tc, x, rel, mean_rel, prec_rel, w, offs, out
                         nc.tensor.matmul(exponent[:], minus_identity[:], dist[:, n, lo:hi], start=True, stop=False)
                         nc.tensor.matmul(exponent[:], level_factor[:], level[:, lo:hi], start=False, stop=True)
                         nc.scalar.activation(gauss[:, n, lo:hi], exponent[:], ACT.Exp)
-                log_total = soft.tile([P, width], F32, name="log_total")
+                log_total = soft.tile([P, width], F32, name="log_total", tag="row")
                 for lo, hi in chunks:
                     total = banks.tile([P, hi - lo], F32, name="total", tag="bank")
                     for n in range(NK):

@@ -16,9 +16,11 @@ D_BLOCKS = D // P
 O_BLOCKS = OP // P
 BANK = 512
 SOFTEN = 16.0
+LEVEL_SLOPE = -SOFTEN * math.log(2.0) / 2**23
+LEVEL_SHIFT = SOFTEN * math.log(2.0) * 127
 PIECES = (512, 1024, 1024, 512)
 assert sum(PIECES) == N and all(width % 32 == 0 for width in PIECES)
-VECTOR_DOES = ("all", "some", "product", "none")
+VECTOR_DOES = ("all", "some", "none", "none")
 
 FLOPS = 2 * D * NK * OP * N
 
@@ -33,17 +35,18 @@ def tile_visualconvolution_b_kernel(tc, x, rel, mean_rel, prec_rel, w, offs, out
     with (
         tc.tile_pool(name="held", bufs=1) as held,
         tc.tile_pool(name="weights", bufs=2) as weights,
-        tc.tile_pool(name="soft", bufs=1) as soft,
+        tc.tile_pool(name="soft", bufs=2) as soft,
+        tc.tile_pool(name="totals", bufs=1) as totals,
         tc.tile_pool(name="products", bufs=6) as products,
         tc.tile_pool(name="rounded", bufs=13) as rounded,
         tc.tile_pool(name="staging", bufs=3) as staging,
-        tc.psum_pool(name="banks", bufs=4) as banks,
-        tc.psum_pool(name="accs", bufs=4) as accs,
+        tc.psum_pool(name="banks", bufs=2) as banks,
+        tc.psum_pool(name="accs", bufs=6) as accs,
     ):
-        mean_all = held.tile([P, NK], F32, name="mean_all")
-        nc.scalar.dma_start(mean_all[:], mean_rel.broadcast_to([P, NK]))
         width_all = held.tile([P, NK], F32, name="width_all")
-        nc.scalar.dma_start(width_all[:], prec_rel.broadcast_to([P, NK]))
+        nc.sync.dma_start(width_all[:], prec_rel.broadcast_to([P, NK]))
+        mean_all = held.tile([P, NK], F32, name="mean_all")
+        nc.sync.dma_start(mean_all[:], mean_rel.broadcast_to([P, NK]))
         rel_sb = held.tile([P, N], F32, name="rel_sb")
         nc.sync.dma_start(rel_sb[:, 0 : PIECES[0]], rel[:, 0 : PIECES[0]])
         offsets = held.tile([P, N // 16], U16, name="offsets")
@@ -67,88 +70,89 @@ def tile_visualconvolution_b_kernel(tc, x, rel, mean_rel, prec_rel, w, offs, out
         nc.vector.tensor_scalar_mul(minus_identity[:], identity[:], -1.0)
         identity_bf = held.tile([P, P], BF16, name="identity_bf")
         nc.vector.tensor_copy(identity_bf[:], identity[:])
-        minus_soften_bf = held.tile([P, P], BF16, name="minus_soften_bf")
-        nc.vector.tensor_scalar_mul(minus_soften_bf[:], identity[:], -SOFTEN)
         inv_width = held.tile([P, NK], F32, name="inv_width")
         nc.vector.reciprocal(inv_width[:], width_all[:])
         slope = held.tile([P, NK], F32, name="slope")
         nc.vector.tensor_scalar_mul(slope[:], inv_width[:], math.sqrt(0.5))
-        neg_mean = held.tile([P, NK], F32, name="neg_mean")
-        nc.vector.tensor_scalar_mul(neg_mean[:], mean_all[:], -1.0)
         shift = held.tile([P, NK], F32, name="shift")
-        nc.vector.tensor_tensor(shift[:], neg_mean[:], slope[:], ALU.mult)
+        nc.vector.scalar_tensor_tensor(shift[:], mean_all[:], -1.0, slope[:], ALU.mult, ALU.mult)
 
         def relation_weights(start, width, vector_does):
             chunks = bank_chunks(width)
-            dist = soft.tile([P, NK, width], F32, name="dist")
-            for n in range(NK):
-                nc.scalar.activation(
-                    dist[:, n, :],
-                    rel_sb[:, start : start + width],
-                    ACT.Square,
-                    bias=shift[:, n : n + 1],
-                    scale=slope[:, n : n + 1],
-                )
-            level = soft.tile([P, width], BF16, name="level")
-            if vector_does in ("product", "none"):
-                level_factor = minus_soften_bf
-                flat = soft.tile([P, NK, width], BF16, name="flat", tag="share")
+            dist = []
+            for c, (lo, hi) in enumerate(chunks):
+                dist.append(soft.tile([P, NK, hi - lo], F32, name="dist"))
                 for n in range(NK):
-                    nc.scalar.activation(flat[:, n, :], dist[:, n, :], ACT.Exp, scale=-1.0 / SOFTEN)
-                for lo, hi in chunks:
+                    nc.scalar.activation(
+                        dist[c][:, n, :],
+                        rel_sb[:, start + lo : start + hi],
+                        ACT.Square,
+                        bias=shift[:, n : n + 1],
+                        scale=slope[:, n : n + 1],
+                    )
+            level = [soft.tile([P, hi - lo], BF16, name="level") for lo, hi in chunks]
+            if vector_does in ("product", "none"):
+                flat = [soft.tile([P, NK, hi - lo], BF16, name="flat", tag="share") for lo, hi in chunks]
+                for c in range(len(chunks)):
+                    for n in range(NK):
+                        nc.scalar.activation(flat[c][:, n, :], dist[c][:, n, :], ACT.Exp, scale=-1.0 / SOFTEN)
+                for c, (lo, hi) in enumerate(chunks):
                     flat_total = banks.tile([P, hi - lo], F32, name="flat_total", tag="bank")
                     for n in range(NK):
-                        nc.tensor.matmul(flat_total[:], identity_bf[:], flat[:, n, lo:hi], start=(n == 0), stop=(n == NK - 1))
-                    nc.scalar.activation(level[:, lo:hi], flat_total[:], ACT.Ln)
+                        nc.tensor.matmul(flat_total[:], identity_bf[:], flat[c][:, n, :], start=(n == 0), stop=(n == NK - 1))
+                    flat_sb = soft.tile([P, hi - lo], F32, name="flat_sb", tag="row")
+                    nc.scalar.copy(flat_sb[:], flat_total[:])
+                    nc.scalar.activation(
+                        level[c][:], flat_sb[:].bitcast(mybir.dt.uint32), ACT.Copy, bias=LEVEL_SHIFT, scale=LEVEL_SLOPE
+                    )
             else:
-                level_factor = identity_bf
-                nearest = soft.tile([P, width], F32, name="nearest", tag="row")
-                nc.vector.tensor_tensor(nearest[:], dist[:, 0, :], dist[:, 1, :], ALU.min)
-                nc.vector.tensor_tensor(nearest[:], nearest[:], dist[:, 2, :], ALU.min)
-                nc.vector.tensor_tensor(level[:], nearest[:], dist[:, 3, :], ALU.min)
-            gauss = soft.tile([P, NK, width], F32, name="gauss")
-            share = soft.tile([P, NK, width], BF16, name="share")
-            if vector_does == "all":
+                for c, (lo, hi) in enumerate(chunks):
+                    nearest = soft.tile([P, hi - lo], F32, name="nearest", tag="row")
+                    nc.vector.tensor_tensor(nearest[:], dist[c][:, 0, :], dist[c][:, 1, :], ALU.min)
+                    nc.vector.tensor_tensor(nearest[:], nearest[:], dist[c][:, 2, :], ALU.min)
+                    nc.vector.tensor_tensor(level[c][:], nearest[:], dist[c][:, 3, :], ALU.min)
+            gauss = []
+            for c, (lo, hi) in enumerate(chunks):
+                gauss.append(soft.tile([P, NK, hi - lo], F32, name="gauss"))
                 for n in range(NK):
-                    nc.vector.tensor_tensor(dist[:, n, :], level[:], dist[:, n, :], ALU.subtract)
-                    nc.scalar.activation(gauss[:, n, :], dist[:, n, :], ACT.Exp)
-                total_sb = soft.tile([P, width], F32, name="total_sb", tag="row")
-                nc.vector.tensor_tensor(total_sb[:], gauss[:, 0, :], gauss[:, 1, :], ALU.add)
-                for n in range(2, NK):
-                    nc.vector.tensor_tensor(total_sb[:], total_sb[:], gauss[:, n, :], ALU.add)
-                inv_total = soft.tile([P, width], F32, name="inv_total")
-                nc.vector.reciprocal(inv_total[:], total_sb[:])
-            else:
-                for lo, hi in chunks:
-                    for n in range(NK):
+                    if vector_does == "all":
+                        nc.vector.tensor_tensor(dist[c][:, n, :], level[c][:], dist[c][:, n, :], ALU.subtract)
+                        nc.scalar.activation(gauss[c][:, n, :], dist[c][:, n, :], ACT.Exp)
+                    else:
                         exponent = banks.tile([P, hi - lo], F32, name="exponent", tag="bank")
-                        nc.tensor.matmul(exponent[:], minus_identity[:], dist[:, n, lo:hi], start=True, stop=False)
-                        nc.tensor.matmul(exponent[:], level_factor[:], level[:, lo:hi], start=False, stop=True)
-                        nc.scalar.activation(gauss[:, n, lo:hi], exponent[:], ACT.Exp)
-                log_total = soft.tile([P, width], F32, name="log_total", tag="row")
-                for lo, hi in chunks:
+                        nc.tensor.matmul(exponent[:], minus_identity[:], dist[c][:, n, :], start=True, stop=False)
+                        nc.tensor.matmul(exponent[:], identity_bf[:], level[c][:], start=False, stop=True)
+                        nc.scalar.activation(gauss[c][:, n, :], exponent[:], ACT.Exp)
+            inv_total = totals.tile([P, width], F32, name="inv_total")
+            log_total = inv_total
+            for c, (lo, hi) in enumerate(chunks):
+                if vector_does == "all":
+                    total_sb = soft.tile([P, hi - lo], F32, name="total_sb", tag="row")
+                    nc.vector.tensor_tensor(total_sb[:], gauss[c][:, 0, :], gauss[c][:, 1, :], ALU.add)
+                    for n in range(2, NK):
+                        nc.vector.tensor_tensor(total_sb[:], total_sb[:], gauss[c][:, n, :], ALU.add)
+                    nc.vector.reciprocal(inv_total[:, lo:hi], total_sb[:])
+                else:
                     total = banks.tile([P, hi - lo], F32, name="total", tag="bank")
                     for n in range(NK):
-                        nc.tensor.matmul(total[:], identity[:], gauss[:, n, lo:hi], start=(n == 0), stop=(n == NK - 1))
+                        nc.tensor.matmul(total[:], identity[:], gauss[c][:, n, :], start=(n == 0), stop=(n == NK - 1))
                     nc.scalar.activation(log_total[:, lo:hi], total[:], ACT.Ln)
-                if vector_does in ("some", "product"):
-                    inv_total = soft.tile([P, width], F32, name="inv_total")
-                    nc.scalar.activation(inv_total[:], log_total[:], ACT.Exp, scale=-1.0)
-            for n in range(NK):
-                if vector_does == "none":
-                    for lo, hi in chunks:
-                        exponent = banks.tile([P, hi - lo], F32, name="exponent", tag="bank")
-                        nc.tensor.matmul(exponent[:], minus_identity[:], dist[:, n, lo:hi], start=True, stop=False)
-                        nc.tensor.matmul(exponent[:], level_factor[:], level[:, lo:hi], start=False, stop=False)
-                        nc.tensor.matmul(exponent[:], minus_identity[:], log_total[:, lo:hi], start=False, stop=True)
-                        nc.scalar.activation(share[:, n, lo:hi], exponent[:], ACT.Exp)
-                else:
-                    nc.vector.tensor_tensor(share[:, n, :], gauss[:, n, :], inv_total[:], ALU.mult)
+            if vector_does in ("some", "product"):
+                nc.scalar.activation(inv_total[:], log_total[:], ACT.Exp, scale=-1.0)
+            share = [soft.tile([P, NK, hi - lo], BF16, name="share") for lo, hi in chunks]
             ws = weights.tile([P, NK, width], F32, name="ws")
             for n in range(NK):
-                for lo, hi in chunks:
+                for c, (lo, hi) in enumerate(chunks):
+                    if vector_does == "none":
+                        exponent = banks.tile([P, hi - lo], F32, name="exponent", tag="bank")
+                        nc.tensor.matmul(exponent[:], minus_identity[:], dist[c][:, n, :], start=True, stop=False)
+                        nc.tensor.matmul(exponent[:], identity_bf[:], level[c][:], start=False, stop=False)
+                        nc.tensor.matmul(exponent[:], minus_identity[:], log_total[:, lo:hi], start=False, stop=True)
+                        nc.scalar.activation(share[c][:, n, :], exponent[:], ACT.Exp)
+                    else:
+                        nc.vector.tensor_tensor(share[c][:, n, :], gauss[c][:, n, :], inv_total[:, lo:hi], ALU.mult)
                     ws_bank = banks.tile([P, hi - lo], F32, name="ws_bank", tag="bank")
-                    nc.tensor.matmul(ws_bank[:], ones[:], share[:, n, lo:hi], start=True, stop=True)
+                    nc.tensor.matmul(ws_bank[:], ones[:], share[c][:, n, :], start=True, stop=True)
                     nc.scalar.copy(ws[:, n, lo:hi], ws_bank[:])
             return ws
 

@@ -20,7 +20,7 @@ LEVEL_SLOPE = -SOFTEN * math.log(2.0) / 2**23
 LEVEL_SHIFT = SOFTEN * math.log(2.0) * 127
 PIECES = (512, 1024, 1024, 512)
 assert sum(PIECES) == N and all(width % 32 == 0 for width in PIECES)
-VECTOR_DOES = ("all", "some", "none", "none")
+VECTOR_DOES = {1: "some", 2: "none", 3: "none"}
 
 FLOPS = 2 * D * NK * OP * N
 
@@ -77,6 +77,44 @@ def tile_visualconvolution_b_kernel(tc, x, rel, mean_rel, prec_rel, w, offs, out
         shift = held.tile([P, NK], F32, name="shift")
         nc.vector.scalar_tensor_tensor(shift[:], mean_all[:], -1.0, slope[:], ALU.mult, ALU.mult)
 
+        def first_weights(width):
+            ws = weights.tile([P, NK, width], F32, name="ws")
+            halves = [(0, width // 2), (width // 2, width)]
+            dist, level, gauss, inv_total, share = {}, {}, {}, {}, {}
+            for lo, hi in halves:
+                dist[lo] = products.tile([P, NK, hi - lo], F32, name="dist", tag="y")
+                for n in range(NK):
+                    nc.scalar.activation(
+                        dist[lo][:, n, :], rel_sb[:, lo:hi], ACT.Square, bias=shift[:, n : n + 1], scale=slope[:, n : n + 1]
+                    )
+            for lo, hi in halves:
+                level[lo] = soft.tile([P, hi - lo], BF16, name="level")
+                nearest = soft.tile([P, hi - lo], F32, name="nearest", tag="row")
+                nc.vector.tensor_tensor(nearest[:], dist[lo][:, 0, :], dist[lo][:, 1, :], ALU.min)
+                nc.vector.tensor_tensor(nearest[:], nearest[:], dist[lo][:, 2, :], ALU.min)
+                nc.vector.tensor_tensor(level[lo][:], nearest[:], dist[lo][:, 3, :], ALU.min)
+            for lo, hi in halves:
+                gauss[lo] = products.tile([P, NK, hi - lo], F32, name="gauss", tag="y")
+                for n in range(NK):
+                    nc.vector.tensor_tensor(dist[lo][:, n, :], level[lo][:], dist[lo][:, n, :], ALU.subtract)
+                    nc.scalar.activation(gauss[lo][:, n, :], dist[lo][:, n, :], ACT.Exp)
+            for lo, hi in halves:
+                total_sb = soft.tile([P, hi - lo], F32, name="total_sb", tag="row")
+                nc.vector.tensor_tensor(total_sb[:], gauss[lo][:, 0, :], gauss[lo][:, 1, :], ALU.add)
+                for n in range(2, NK):
+                    nc.vector.tensor_tensor(total_sb[:], total_sb[:], gauss[lo][:, n, :], ALU.add)
+                inv_total[lo] = products.tile([P, hi - lo], F32, name="inv_total", tag="y")
+                nc.vector.reciprocal(inv_total[lo][:], total_sb[:])
+            for n in range(NK):
+                for lo, hi in halves:
+                    if n == 0:
+                        share[lo] = soft.tile([P, NK, hi - lo], BF16, name="share")
+                    nc.vector.tensor_tensor(share[lo][:, n, :], gauss[lo][:, n, :], inv_total[lo][:], ALU.mult)
+                    ws_bank = banks.tile([P, hi - lo], F32, name="ws_bank", tag="bank")
+                    nc.tensor.matmul(ws_bank[:], ones[:], share[lo][:, n, :], start=True, stop=True)
+                    nc.scalar.copy(ws[:, n, lo:hi], ws_bank[:])
+            return ws
+
         def relation_weights(start, width, vector_does):
             chunks = bank_chunks(width)
             dist = []
@@ -91,7 +129,7 @@ def tile_visualconvolution_b_kernel(tc, x, rel, mean_rel, prec_rel, w, offs, out
                         scale=slope[:, n : n + 1],
                     )
             level = [soft.tile([P, hi - lo], BF16, name="level") for lo, hi in chunks]
-            if vector_does in ("product", "none"):
+            if vector_does == "none":
                 flat = [soft.tile([P, NK, hi - lo], BF16, name="flat", tag="share") for lo, hi in chunks]
                 for c in range(len(chunks)):
                     for n in range(NK):
@@ -115,29 +153,18 @@ def tile_visualconvolution_b_kernel(tc, x, rel, mean_rel, prec_rel, w, offs, out
             for c, (lo, hi) in enumerate(chunks):
                 gauss.append(soft.tile([P, NK, hi - lo], F32, name="gauss"))
                 for n in range(NK):
-                    if vector_does == "all":
-                        nc.vector.tensor_tensor(dist[c][:, n, :], level[c][:], dist[c][:, n, :], ALU.subtract)
-                        nc.scalar.activation(gauss[c][:, n, :], dist[c][:, n, :], ACT.Exp)
-                    else:
-                        exponent = banks.tile([P, hi - lo], F32, name="exponent", tag="bank")
-                        nc.tensor.matmul(exponent[:], minus_identity[:], dist[c][:, n, :], start=True, stop=False)
-                        nc.tensor.matmul(exponent[:], identity_bf[:], level[c][:], start=False, stop=True)
-                        nc.scalar.activation(gauss[c][:, n, :], exponent[:], ACT.Exp)
+                    exponent = banks.tile([P, hi - lo], F32, name="exponent", tag="bank")
+                    nc.tensor.matmul(exponent[:], minus_identity[:], dist[c][:, n, :], start=True, stop=False)
+                    nc.tensor.matmul(exponent[:], identity_bf[:], level[c][:], start=False, stop=True)
+                    nc.scalar.activation(gauss[c][:, n, :], exponent[:], ACT.Exp)
             inv_total = totals.tile([P, width], F32, name="inv_total")
             log_total = inv_total
             for c, (lo, hi) in enumerate(chunks):
-                if vector_does == "all":
-                    total_sb = soft.tile([P, hi - lo], F32, name="total_sb", tag="row")
-                    nc.vector.tensor_tensor(total_sb[:], gauss[c][:, 0, :], gauss[c][:, 1, :], ALU.add)
-                    for n in range(2, NK):
-                        nc.vector.tensor_tensor(total_sb[:], total_sb[:], gauss[c][:, n, :], ALU.add)
-                    nc.vector.reciprocal(inv_total[:, lo:hi], total_sb[:])
-                else:
-                    total = banks.tile([P, hi - lo], F32, name="total", tag="bank")
-                    for n in range(NK):
-                        nc.tensor.matmul(total[:], identity[:], gauss[c][:, n, :], start=(n == 0), stop=(n == NK - 1))
-                    nc.scalar.activation(log_total[:, lo:hi], total[:], ACT.Ln)
-            if vector_does in ("some", "product"):
+                total = banks.tile([P, hi - lo], F32, name="total", tag="bank")
+                for n in range(NK):
+                    nc.tensor.matmul(total[:], identity[:], gauss[c][:, n, :], start=(n == 0), stop=(n == NK - 1))
+                nc.scalar.activation(log_total[:, lo:hi], total[:], ACT.Ln)
+            if vector_does == "some":
                 nc.scalar.activation(inv_total[:], log_total[:], ACT.Exp, scale=-1.0)
             share = [soft.tile([P, NK, hi - lo], BF16, name="share") for lo, hi in chunks]
             ws = weights.tile([P, NK, width], F32, name="ws")
@@ -183,7 +210,7 @@ def tile_visualconvolution_b_kernel(tc, x, rel, mean_rel, prec_rel, w, offs, out
                         nc.scalar.copy(staged[:, lo:hi], acc[o][c][:])
                     nc.sync.dma_start(out[first : first + P, start : start + width], staged[:])
 
-        ws_next = relation_weights(starts[0], PIECES[0], VECTOR_DOES[0])
+        ws_next = first_weights(PIECES[0])
         for i, width in enumerate(PIECES):
             ws_now = ws_next
             if i + 1 < len(PIECES):

@@ -37,9 +37,9 @@ def tile_visualconvolution_b_kernel(tc, x, rel, mean_rel, prec_rel, w, offs, out
         tc.tile_pool(name="weights", bufs=2) as weights,
         tc.tile_pool(name="soft", bufs=2) as soft,
         tc.tile_pool(name="totals", bufs=1) as totals,
-        tc.tile_pool(name="products", bufs=6) as products,
+        tc.tile_pool(name="products", bufs=7) as products,
         tc.tile_pool(name="rounded", bufs=13) as rounded,
-        tc.tile_pool(name="staging", bufs=3) as staging,
+        tc.tile_pool(name="staging", bufs=2) as staging,
         tc.psum_pool(name="banks", bufs=2) as banks,
         tc.psum_pool(name="accs", bufs=6) as accs,
     ):

import math

import concourse.mybir as mybir
from concourse.masks import make_identity

F32 = mybir.dt.float32
BF16 = mybir.dt.bfloat16
U16 = mybir.dt.uint16
ALU = mybir.AluOpType
ACT = mybir.ActivationFunctionType

P = 128
D, S, N = 1024, 2048, 3072
NK, OP = 4, 256
D_BLOCKS = D // P
O_BLOCKS = OP // P
BANK = 512
SOFTEN = 16.0
LEVEL_SLOPE = -SOFTEN * math.log(2.0) / 2**23
LEVEL_SHIFT = SOFTEN * math.log(2.0) * 127
PIECES = (512, 1024, 1024, 512)
assert sum(PIECES) == N and all(width % 32 == 0 for width in PIECES)
VECTOR_DOES = {1: "some", 2: "none", 3: "none"}

FLOPS = 2 * D * NK * OP * N


def bank_chunks(width):
    return [(lo, min(lo + BANK, width)) for lo in range(0, width, BANK)]


def tile_visualconvolution_b_kernel(tc, x, rel, mean_rel, prec_rel, w, offs, out):
    nc = tc.nc
    starts = [sum(PIECES[:i]) for i in range(len(PIECES))]
    with (
        tc.tile_pool(name="held", bufs=1) as held,
        tc.tile_pool(name="weights", bufs=2) as weights,
        tc.tile_pool(name="soft", bufs=2) as soft,
        tc.tile_pool(name="totals", bufs=1) as totals,
        tc.tile_pool(name="products", bufs=7) as products,
        tc.tile_pool(name="rounded", bufs=13) as rounded,
        tc.tile_pool(name="staging", bufs=2) as staging,
        tc.psum_pool(name="banks", bufs=2) as banks,
        tc.psum_pool(name="accs", bufs=6) as accs,
    ):
        width_all = held.tile([P, NK], F32, name="width_all")
        nc.sync.dma_start(width_all[:], prec_rel.broadcast_to([P, NK]))
        mean_all = held.tile([P, NK], F32, name="mean_all")
        nc.sync.dma_start(mean_all[:], mean_rel.broadcast_to([P, NK]))
        rel_sb = held.tile([P, N], F32, name="rel_sb")
        nc.sync.dma_start(rel_sb[:, 0 : PIECES[0]], rel[:, 0 : PIECES[0]])
        offsets = held.tile([P, N // 16], U16, name="offsets")
        nc.sync.dma_start(offsets[:], offs)
        x_blocks = [held.tile([P, S], F32, name=f"x{b}") for b in range(D_BLOCKS)]
        w_sb = held.tile([P, D_BLOCKS, NK * OP], BF16, name="w_sb")
        for b in range(D_BLOCKS):
            nc.sync.dma_start(x_blocks[b][:], x[b * P : (b + 1) * P, :])
            nc.sync.dma_start(w_sb[:, b, :], w[b * P : (b + 1) * P, :])
            if b + 1 < len(PIECES):
                later = slice(starts[b + 1], starts[b + 1] + PIECES[b + 1])
                nc.sync.dma_start(rel_sb[:, later], rel[:, later])

        ones = held.tile([P, P], BF16, name="ones")
        nc.gpsimd.memset(ones[:], 1.0)
        warm = held.tile([P, 1], F32, name="warm")
        nc.scalar.activation(warm[:], ones[:, 0:1], ACT.Exp)
        identity = held.tile([P, P], F32, name="identity")
        make_identity(nc, identity[:])
        minus_identity = held.tile([P, P], F32, name="minus_identity")
        nc.vector.tensor_scalar_mul(minus_identity[:], identity[:], -1.0)
        identity_bf = held.tile([P, P], BF16, name="identity_bf")
        nc.vector.tensor_copy(identity_bf[:], identity[:])
        inv_width = held.tile([P, NK], F32, name="inv_width")
        nc.vector.reciprocal(inv_width[:], width_all[:])
        slope = held.tile([P, NK], F32, name="slope")
        nc.vector.tensor_scalar_mul(slope[:], inv_width[:], math.sqrt(0.5))
        shift = held.tile([P, NK], F32, name="shift")
        nc.vector.scalar_tensor_tensor(shift[:], mean_all[:], -1.0, slope[:], ALU.mult, ALU.mult)

        def first_weights(width):
            ws = weights.tile([P, NK, width], F32, name="ws")
            halves = [(0, width // 2), (width // 2, width)]
            dist, level, gauss, inv_total, share = {}, {}, {}, {}, {}
            for lo, hi in halves:
                dist[lo] = products.tile([P, NK, hi - lo], F32, name="dist", tag="y")
                for n in range(NK):
                    nc.scalar.activation(
                        dist[lo][:, n, :], rel_sb[:, lo:hi], ACT.Square, bias=shift[:, n : n + 1], scale=slope[:, n : n + 1]
                    )
            for lo, hi in halves:
                level[lo] = soft.tile([P, hi - lo], BF16, name="level")
                nearest = soft.tile([P, hi - lo], F32, name="nearest", tag="row")
                nc.vector.tensor_tensor(nearest[:], dist[lo][:, 0, :], dist[lo][:, 1, :], ALU.min)
                nc.vector.tensor_tensor(nearest[:], nearest[:], dist[lo][:, 2, :], ALU.min)
                nc.vector.tensor_tensor(level[lo][:], nearest[:], dist[lo][:, 3, :], ALU.min)
            for lo, hi in halves:
                gauss[lo] = products.tile([P, NK, hi - lo], F32, name="gauss", tag="y")
                for n in range(NK):
                    nc.vector.tensor_tensor(dist[lo][:, n, :], level[lo][:], dist[lo][:, n, :], ALU.subtract)
                    nc.scalar.activation(gauss[lo][:, n, :], dist[lo][:, n, :], ACT.Exp)
            for lo, hi in halves:
                total_sb = soft.tile([P, hi - lo], F32, name="total_sb", tag="row")
                nc.vector.tensor_tensor(total_sb[:], gauss[lo][:, 0, :], gauss[lo][:, 1, :], ALU.add)
                for n in range(2, NK):
                    nc.vector.tensor_tensor(total_sb[:], total_sb[:], gauss[lo][:, n, :], ALU.add)
                inv_total[lo] = products.tile([P, hi - lo], F32, name="inv_total", tag="y")
                nc.vector.reciprocal(inv_total[lo][:], total_sb[:])
            for n in range(NK):
                for lo, hi in halves:
                    if n == 0:
                        share[lo] = soft.tile([P, NK, hi - lo], BF16, name="share")
                    nc.vector.tensor_tensor(share[lo][:, n, :], gauss[lo][:, n, :], inv_total[lo][:], ALU.mult)
                    ws_bank = banks.tile([P, hi - lo], F32, name="ws_bank", tag="bank")
                    nc.tensor.matmul(ws_bank[:], ones[:], share[lo][:, n, :], start=True, stop=True)
                    nc.scalar.copy(ws[:, n, lo:hi], ws_bank[:])
            return ws

        def relation_weights(start, width, vector_does):
            chunks = bank_chunks(width)
            dist = []
            for c, (lo, hi) in enumerate(chunks):
                dist.append(soft.tile([P, NK, hi - lo], F32, name="dist"))
                for n in range(NK):
                    nc.scalar.activation(
                        dist[c][:, n, :],
                        rel_sb[:, start + lo : start + hi],
                        ACT.Square,
                        bias=shift[:, n : n + 1],
                        scale=slope[:, n : n + 1],
                    )
            level = [soft.tile([P, hi - lo], BF16, name="level") for lo, hi in chunks]
            if vector_does == "none":
                flat = [soft.tile([P, NK, hi - lo], BF16, name="flat", tag="share") for lo, hi in chunks]
                for c in range(len(chunks)):
                    for n in range(NK):
                        nc.scalar.activation(flat[c][:, n, :], dist[c][:, n, :], ACT.Exp, scale=-1.0 / SOFTEN)
                for c, (lo, hi) in enumerate(chunks):
                    flat_total = banks.tile([P, hi - lo], F32, name="flat_total", tag="bank")
                    for n in range(NK):
                        nc.tensor.matmul(flat_total[:], identity_bf[:], flat[c][:, n, :], start=(n == 0), stop=(n == NK - 1))
                    flat_sb = soft.tile([P, hi - lo], F32, name="flat_sb", tag="row")
                    nc.scalar.copy(flat_sb[:], flat_total[:])
                    nc.scalar.activation(
                        level[c][:], flat_sb[:].bitcast(mybir.dt.uint32), ACT.Copy, bias=LEVEL_SHIFT, scale=LEVEL_SLOPE
                    )
            else:
                for c, (lo, hi) in enumerate(chunks):
                    nearest = soft.tile([P, hi - lo], F32, name="nearest", tag="row")
                    nc.vector.tensor_tensor(nearest[:], dist[c][:, 0, :], dist[c][:, 1, :], ALU.min)
                    nc.vector.tensor_tensor(nearest[:], nearest[:], dist[c][:, 2, :], ALU.min)
                    nc.vector.tensor_tensor(level[c][:], nearest[:], dist[c][:, 3, :], ALU.min)
            gauss = []
            for c, (lo, hi) in enumerate(chunks):
                gauss.append(soft.tile([P, NK, hi - lo], F32, name="gauss"))
                for n in range(NK):
                    exponent = banks.tile([P, hi - lo], F32, name="exponent", tag="bank")
                    nc.tensor.matmul(exponent[:], minus_identity[:], dist[c][:, n, :], start=True, stop=False)
                    nc.tensor.matmul(exponent[:], identity_bf[:], level[c][:], start=False, stop=True)
                    nc.scalar.activation(gauss[c][:, n, :], exponent[:], ACT.Exp)
            inv_total = totals.tile([P, width], F32, name="inv_total")
            log_total = inv_total
            for c, (lo, hi) in enumerate(chunks):
                total = banks.tile([P, hi - lo], F32, name="total", tag="bank")
                for n in range(NK):
                    nc.tensor.matmul(total[:], identity[:], gauss[c][:, n, :], start=(n == 0), stop=(n == NK - 1))
                nc.scalar.activation(log_total[:, lo:hi], total[:], ACT.Ln)
            if vector_does == "some":
                nc.scalar.activation(inv_total[:], log_total[:], ACT.Exp, scale=-1.0)
            share = [soft.tile([P, NK, hi - lo], BF16, name="share") for lo, hi in chunks]
            ws = weights.tile([P, NK, width], F32, name="ws")
            for n in range(NK):
                for c, (lo, hi) in enumerate(chunks):
                    if vector_does == "none":
                        exponent = banks.tile([P, hi - lo], F32, name="exponent", tag="bank")
                        nc.tensor.matmul(exponent[:], minus_identity[:], dist[c][:, n, :], start=True, stop=False)
                        nc.tensor.matmul(exponent[:], identity_bf[:], level[c][:], start=False, stop=False)
                        nc.tensor.matmul(exponent[:], minus_identity[:], log_total[:, lo:hi], start=False, stop=True)
                        nc.scalar.activation(share[c][:, n, :], exponent[:], ACT.Exp)
                    else:
                        nc.vector.tensor_tensor(share[c][:, n, :], gauss[c][:, n, :], inv_total[:, lo:hi], ALU.mult)
                    ws_bank = banks.tile([P, hi - lo], F32, name="ws_bank", tag="bank")
                    nc.tensor.matmul(ws_bank[:], ones[:], share[c][:, n, :], start=True, stop=True)
                    nc.scalar.copy(ws[:, n, lo:hi], ws_bank[:])
            return ws

        def convolve(start, width, ws):
            chunks = bank_chunks(width)
            piece_offsets = offsets[:, start // 16 : (start + width) // 16]
            for n in range(NK):
                acc = [[accs.tile([P, hi - lo], F32, name="acc") for lo, hi in chunks] for o in range(O_BLOCKS)]
                for b in range(D_BLOCKS):
                    y = products.tile([P, width], F32, name="y")
                    nc.vector.tensor_tensor(y[:], x_blocks[b][:].indirect(piece_offsets), ws[:, n, :], ALU.mult)
                    y_bf = rounded.tile([P, width], BF16, name="y_bf")
                    nc.scalar.copy(y_bf[:], y[:])
                    for o in range(O_BLOCKS):
                        first = n * OP + o * P
                        for c, (lo, hi) in enumerate(chunks):
                            nc.tensor.matmul(
                                acc[o][c][:],
                                w_sb[:, b, first : first + P],
                                y_bf[:, lo:hi],
                                start=(b == 0),
                                stop=(b == D_BLOCKS - 1),
                            )
                for o in range(O_BLOCKS):
                    first = n * OP + o * P
                    staged = staging.tile([P, width], F32, name="staged")
                    for c, (lo, hi) in enumerate(chunks):
                        nc.scalar.copy(staged[:, lo:hi], acc[o][c][:])
                    nc.sync.dma_start(out[first : first + P, start : start + width], staged[:])

        ws_next = first_weights(PIECES[0])
        for i, width in enumerate(PIECES):
            ws_now = ws_next
            if i + 1 < len(PIECES):
                ws_next = relation_weights(starts[i + 1], PIECES[i + 1], VECTOR_DOES[i + 1])
            convolve(starts[i], width, ws_now)
